import numpy as np
import ml_dtypes

BF16 = ml_dtypes.bfloat16


def bf(x):
    return np.asarray(x, np.float32).astype(BF16)


def f32(x):
    return np.asarray(x, np.float32)


def f64(x):
    return np.asarray(x).astype(np.float64)


def striped(idx):
    return np.tile(idx.reshape(-1, 16).T, (8, 1))


K, S, NV, N, H, R, Q = 128, 256, 4, 1024, 128, 256, 128


def setup_inputs():
    idx = np.concatenate([np.random.permutation(S)[:H] for _ in range(N // H)])
    return {"table": bf(np.random.standard_normal((K, S))), "w1": bf(np.random.standard_normal((K, R)) / np.sqrt(K)), "vproj": f32(np.random.standard_normal((R, NV))), "b1": f32(0.1 * np.random.standard_normal((R, 1))), "w2": bf(np.random.standard_normal((R, Q)) / np.sqrt(R)), "b2": f32(0.1 * np.random.standard_normal((Q, 1))), "offs": striped(idx)}


def reference(table, w1, vproj, b1, w2, b2, offs):
    idx = offs[:16].T.reshape(-1)
    h = np.maximum(f64(w1).T @ f64(table)[:, idx] + np.repeat(f64(vproj), S, axis=1) + f64(b1), 0.0)
    return np.maximum(f64(w2).T @ h + f64(b2), 0.0)

@@ -1,0 +1,63 @@
+import concourse.mybir as mybir
+
+BF16, F32, U16 = mybir.dt.bfloat16, mybir.dt.float32, mybir.dt.uint16
+ADD, MAX = mybir.AluOpType.add, mybir.AluOpType.max
+RELU = mybir.ActivationFunctionType.Relu
+
+P = 128
+K, S = 128, 256
+R, Q = 256, 128
+N, NV = 1024, 4
+BLOCKS = R // P
+PIECE = N // NV
+COLS = PIECE // 16
+FLOPS = 2 * K * R * N + 2 * R * Q * N
+
+
+def tile_bipartitegraph_kernel(tc, table, w1, vproj, b1, w2, b2, offs, out):
+    nc = tc.nc
+    with (
+        tc.tile_pool(name="held", bufs=1) as held,
+        tc.tile_pool(name="work", bufs=NV) as work,
+        tc.psum_pool(name="psum", bufs=1) as psum,
+    ):
+        offsets = held.tile([P, N // 16], U16, name="offsets")
+        nc.sync.dma_start(offsets[:], offs)
+        table_sb = held.tile([K, S], BF16, name="table_sb")
+        nc.scalar.dma_start(table_sb[:], table)
+        w1_sb = held.tile([K, BLOCKS, P], BF16, name="w1_sb")
+        nc.sync.dma_start(w1_sb[:], w1.rearrange("k (i p) -> k i p", i=BLOCKS))
+        vproj_sb = held.tile([P, BLOCKS, NV], F32, name="vproj_sb")
+        nc.scalar.dma_start(vproj_sb[:], vproj.rearrange("(i p) t -> p i t", i=BLOCKS))
+        b1_sb = held.tile([P, BLOCKS, 1], F32, name="b1_sb")
+        nc.sync.dma_start(b1_sb[:], b1.rearrange("(i p) o -> p i o", i=BLOCKS))
+        w2_sb = held.tile([P, BLOCKS, Q], BF16, name="w2_sb")
+        nc.scalar.dma_start(w2_sb[:], w2.rearrange("(i p) q -> p i q", i=BLOCKS))
+        b2_sb = held.tile([Q, 1], F32, name="b2_sb")
+        nc.sync.dma_start(b2_sb[:], b2)
+
+        bias1 = held.tile([P, BLOCKS, NV], F32, name="bias1")
+        nc.vector.tensor_tensor(bias1[:], vproj_sb[:], b1_sb[:].to_broadcast([P, BLOCKS, NV]), ADD)
+
+        acc_h = [[psum.tile([P, 2, PIECE], F32, name=f"acc_h{i}{pair}") for pair in range(NV // 2)] for i in range(BLOCKS)]
+        for pair in range(NV // 2):
+            for i in range(BLOCKS):
+                for t in (2 * pair, 2 * pair + 1):
+                    looked_up = table_sb[:].indirect(offsets[:, t * COLS : (t + 1) * COLS])
+                    nc.tensor.matmul(acc_h[i][pair][:, t % 2, :], w1_sb[:, i, :], looked_up, start=True, stop=True)
+
+        h = [[work.tile([P, PIECE], BF16, name=f"h{i}") for t in range(NV)] for i in range(BLOCKS)]
+        for t in range(NV):
+            nc.scalar.activation(h[0][t][:], acc_h[0][t // 2][:, t % 2, :], RELU, bias=bias1[:, 0, t : t + 1])
+            nc.vector.tensor_scalar(h[1][t][:], acc_h[1][t // 2][:, t % 2, :], bias1[:, 1, t : t + 1], 0.0, ADD, MAX)
+
+        for t in range(NV):
+            acc_o = psum.tile([Q, PIECE], F32, name=f"acc_o{t}")
+            for i in range(BLOCKS):
+                nc.tensor.matmul(acc_o[:], w2_sb[:, i, :], h[i][t][:], start=(i == 0), stop=(i == BLOCKS - 1))
+            out_sb = work.tile([Q, PIECE], F32, name="out_sb")
+            if t < NV // 2:
+                nc.scalar.activation(out_sb[:], acc_o[:], RELU, bias=b2_sb[:, 0:1])
+            else:
+                nc.vector.tensor_scalar(out_sb[:], acc_o[:], b2_sb[:, 0:1], 0.0, ADD, MAX)
+            nc.sync.dma_start(out[:, t * PIECE : (t + 1) * PIECE], out_sb[:])

@@ -11,6 +11,8 @@ N, NV = 1024, 4
 BLOCKS = R // P
 PIECE = N // NV
 COLS = PIECE // 16
+BANK = 512
+WARM_UPS = 4
 FLOPS = 2 * K * R * N + 2 * R * Q * N
 
 
@@ -36,6 +38,12 @@ def tile_bipartitegraph_kernel(tc, table, w1, vproj, b1, w2, b2, offs, out):
         b2_sb = held.tile([Q, 1], F32, name="b2_sb")
         nc.sync.dma_start(b2_sb[:], b2)
 
+        zeros = held.tile([P, BANK], BF16, name="zeros")
+        nc.vector.memset(zeros[:], 0.0)
+        warm_acc = psum.tile([P, BANK], F32, name="warm_acc", tag=f"acc_o{NV - 1}")
+        for w in range(WARM_UPS):
+            nc.tensor.matmul(warm_acc[:], zeros[:, 0:P], zeros[:], start=True, stop=True)
+
         bias1 = held.tile([P, BLOCKS, NV], F32, name="bias1")
         nc.vector.tensor_tensor(bias1[:], vproj_sb[:], b1_sb[:].to_broadcast([P, BLOCKS, NV]), ADD)
 
@@ -52,7 +60,7 @@ def tile_bipartitegraph_kernel(tc, table, w1, vproj, b1, w2, b2, offs, out):
             nc.vector.tensor_scalar(h[1][t][:], acc_h[1][t // 2][:, t % 2, :], bias1[:, 1, t : t + 1], 0.0, ADD, MAX)
 
         for t in range(NV):
-            acc_o = psum.tile([Q, PIECE], F32, name=f"acc_o{t}")
+            acc_o = psum.tile([Q, PIECE], F32, name=f"acc_o{t}", tag=f"acc_o{t}")
             for i in range(BLOCKS):
                 nc.tensor.matmul(acc_o[:], w2_sb[:, i, :], h[i][t][:], start=(i == 0), stop=(i == BLOCKS - 1))
             out_sb = work.tile([Q, PIECE], F32, name="out_sb")

@@ -11,8 +11,6 @@ N, NV = 1024, 4
 BLOCKS = R // P
 PIECE = N // NV
 COLS = PIECE // 16
-BANK = 512
-WARM_UPS = 4
 FLOPS = 2 * K * R * N + 2 * R * Q * N
 
 
@@ -38,33 +36,26 @@ def tile_bipartitegraph_kernel(tc, table, w1, vproj, b1, w2, b2, offs, out):
         b2_sb = held.tile([Q, 1], F32, name="b2_sb")
         nc.sync.dma_start(b2_sb[:], b2)
 
-        zeros = held.tile([P, BANK], BF16, name="zeros")
-        nc.vector.memset(zeros[:], 0.0)
-        warm_acc = psum.tile([P, BANK], F32, name="warm_acc", tag=f"acc_o{NV - 1}")
-        for w in range(WARM_UPS):
-            nc.tensor.matmul(warm_acc[:], zeros[:, 0:P], zeros[:], start=True, stop=True)
-
         bias1 = held.tile([P, BLOCKS, NV], F32, name="bias1")
         nc.vector.tensor_tensor(bias1[:], vproj_sb[:], b1_sb[:].to_broadcast([P, BLOCKS, NV]), ADD)
 
-        acc_h = [[psum.tile([P, 2, PIECE], F32, name=f"acc_h{i}{pair}") for pair in range(NV // 2)] for i in range(BLOCKS)]
-        for pair in range(NV // 2):
+        acc_h = [[psum.tile([P, PIECE], F32, name=f"acc_h{i}{t}") for t in range(NV)] for i in range(BLOCKS)]
+        for t in range(NV):
+            looked_up = table_sb[:].indirect(offsets[:, t * COLS : (t + 1) * COLS])
             for i in range(BLOCKS):
-                for t in (2 * pair, 2 * pair + 1):
-                    looked_up = table_sb[:].indirect(offsets[:, t * COLS : (t + 1) * COLS])
-                    nc.tensor.matmul(acc_h[i][pair][:, t % 2, :], w1_sb[:, i, :], looked_up, start=True, stop=True)
+                nc.tensor.matmul(acc_h[i][t][:], w1_sb[:, i, :], looked_up, start=True, stop=True)
 
         h = [[work.tile([P, PIECE], BF16, name=f"h{i}") for t in range(NV)] for i in range(BLOCKS)]
         for t in range(NV):
-            nc.scalar.activation(h[0][t][:], acc_h[0][t // 2][:, t % 2, :], RELU, bias=bias1[:, 0, t : t + 1])
-            nc.vector.tensor_scalar(h[1][t][:], acc_h[1][t // 2][:, t % 2, :], bias1[:, 1, t : t + 1], 0.0, ADD, MAX)
+            nc.scalar.activation(h[0][t][:], acc_h[0][t][:], RELU, bias=bias1[:, 0, t : t + 1])
+            nc.vector.tensor_scalar(h[1][t][:], acc_h[1][t][:], bias1[:, 1, t : t + 1], 0.0, ADD, MAX)
 
         for t in range(NV):
-            acc_o = psum.tile([Q, PIECE], F32, name=f"acc_o{t}", tag=f"acc_o{t}")
+            acc_o = psum.tile([Q, PIECE], F32, name=f"acc_o{t}", tag=f"acc_h0{t}")
             for i in range(BLOCKS):
                 nc.tensor.matmul(acc_o[:], w2_sb[:, i, :], h[i][t][:], start=(i == 0), stop=(i == BLOCKS - 1))
             out_sb = work.tile([Q, PIECE], F32, name="out_sb")
-            if t < NV // 2:
+            if t % 2 == 0:
                 nc.scalar.activation(out_sb[:], acc_o[:], RELU, bias=b2_sb[:, 0:1])
             else:
                 nc.vector.tensor_scalar(out_sb[:], acc_o[:], b2_sb[:, 0:1], 0.0, ADD, MAX)

@@ -24,17 +24,17 @@ def tile_bipartitegraph_kernel(tc, table, w1, vproj, b1, w2, b2, offs, out):
         offsets = held.tile([P, N // 16], U16, name="offsets")
         nc.sync.dma_start(offsets[:], offs)
         table_sb = held.tile([K, S], BF16, name="table_sb")
-        nc.scalar.dma_start(table_sb[:], table)
+        nc.sync.dma_start(table_sb[:], table)
         w1_sb = held.tile([K, BLOCKS, P], BF16, name="w1_sb")
         nc.sync.dma_start(w1_sb[:], w1.rearrange("k (i p) -> k i p", i=BLOCKS))
         vproj_sb = held.tile([P, BLOCKS, NV], F32, name="vproj_sb")
-        nc.scalar.dma_start(vproj_sb[:], vproj.rearrange("(i p) t -> p i t", i=BLOCKS))
+        nc.sync.dma_start(vproj_sb[:], vproj.rearrange("(i p) t -> p i t", i=BLOCKS))
         b1_sb = held.tile([P, BLOCKS, 1], F32, name="b1_sb")
         nc.sync.dma_start(b1_sb[:], b1.rearrange("(i p) o -> p i o", i=BLOCKS))
         w2_sb = held.tile([P, BLOCKS, Q], BF16, name="w2_sb")
         nc.scalar.dma_start(w2_sb[:], w2.rearrange("(i p) q -> p i q", i=BLOCKS))
         b2_sb = held.tile([Q, 1], F32, name="b2_sb")
-        nc.sync.dma_start(b2_sb[:], b2)
+        nc.scalar.dma_start(b2_sb[:], b2)
 
         bias1 = held.tile([P, BLOCKS, NV], F32, name="bias1")
         nc.vector.tensor_tensor(bias1[:], vproj_sb[:], b1_sb[:].to_broadcast([P, BLOCKS, NV]), ADD)

@@ -11,6 +11,7 @@ N, NV = 1024, 4
 BLOCKS = R // P
 PIECE = N // NV
 COLS = PIECE // 16
+HALF = PIECE // 2
 FLOPS = 2 * K * R * N + 2 * R * Q * N
 
 
@@ -24,17 +25,17 @@ def tile_bipartitegraph_kernel(tc, table, w1, vproj, b1, w2, b2, offs, out):
         offsets = held.tile([P, N // 16], U16, name="offsets")
         nc.sync.dma_start(offsets[:], offs)
         table_sb = held.tile([K, S], BF16, name="table_sb")
-        nc.sync.dma_start(table_sb[:], table)
+        nc.scalar.dma_start(table_sb[:], table)
         w1_sb = held.tile([K, BLOCKS, P], BF16, name="w1_sb")
         nc.sync.dma_start(w1_sb[:], w1.rearrange("k (i p) -> k i p", i=BLOCKS))
         vproj_sb = held.tile([P, BLOCKS, NV], F32, name="vproj_sb")
-        nc.sync.dma_start(vproj_sb[:], vproj.rearrange("(i p) t -> p i t", i=BLOCKS))
+        nc.scalar.dma_start(vproj_sb[:], vproj.rearrange("(i p) t -> p i t", i=BLOCKS))
         b1_sb = held.tile([P, BLOCKS, 1], F32, name="b1_sb")
         nc.sync.dma_start(b1_sb[:], b1.rearrange("(i p) o -> p i o", i=BLOCKS))
         w2_sb = held.tile([P, BLOCKS, Q], BF16, name="w2_sb")
         nc.scalar.dma_start(w2_sb[:], w2.rearrange("(i p) q -> p i q", i=BLOCKS))
         b2_sb = held.tile([Q, 1], F32, name="b2_sb")
-        nc.scalar.dma_start(b2_sb[:], b2)
+        nc.sync.dma_start(b2_sb[:], b2)
 
         bias1 = held.tile([P, BLOCKS, NV], F32, name="bias1")
         nc.vector.tensor_tensor(bias1[:], vproj_sb[:], b1_sb[:].to_broadcast([P, BLOCKS, NV]), ADD)
@@ -51,12 +52,16 @@ def tile_bipartitegraph_kernel(tc, table, w1, vproj, b1, w2, b2, offs, out):
             nc.vector.tensor_scalar(h[1][t][:], acc_h[1][t][:], bias1[:, 1, t : t + 1], 0.0, ADD, MAX)
 
         for t in range(NV):
-            acc_o = psum.tile([Q, PIECE], F32, name=f"acc_o{t}", tag=f"acc_h0{t}")
-            for i in range(BLOCKS):
-                nc.tensor.matmul(acc_o[:], w2_sb[:, i, :], h[i][t][:], start=(i == 0), stop=(i == BLOCKS - 1))
-            out_sb = work.tile([Q, PIECE], F32, name="out_sb")
-            if t % 2 == 0:
-                nc.scalar.activation(out_sb[:], acc_o[:], RELU, bias=b2_sb[:, 0:1])
-            else:
-                nc.vector.tensor_scalar(out_sb[:], acc_o[:], b2_sb[:, 0:1], 0.0, ADD, MAX)
-            nc.sync.dma_start(out[:, t * PIECE : (t + 1) * PIECE], out_sb[:])
+            acc_o = [psum.tile([Q, HALF], F32, name=f"acc_o{t}{s}", tag=f"acc_h{s}{t}") for s in range(2)]
+            for s in range(2):
+                for i in range(BLOCKS):
+                    nc.tensor.matmul(
+                        acc_o[s][:], w2_sb[:, i, :], h[i][t][:, s * HALF : (s + 1) * HALF],
+                        start=(i == 0), stop=(i == BLOCKS - 1),
+                    )
+            out_left = work.tile([Q, HALF], F32, name="out_left")
+            nc.scalar.activation(out_left[:], acc_o[0][:], RELU, bias=b2_sb[:, 0:1])
+            nc.scalar.dma_start(out[:, t * PIECE : t * PIECE + HALF], out_left[:])
+            out_right = work.tile([Q, HALF], F32, name="out_right")
+            nc.vector.tensor_scalar(out_right[:], acc_o[1][:], b2_sb[:, 0:1], 0.0, ADD, MAX)
+            nc.sync.dma_start(out[:, t * PIECE + HALF : (t + 1) * PIECE], out_right[:])

@@ -11,7 +11,6 @@ N, NV = 1024, 4
 BLOCKS = R // P
 PIECE = N // NV
 COLS = PIECE // 16
-HALF = PIECE // 2
 FLOPS = 2 * K * R * N + 2 * R * Q * N
 
 
@@ -22,12 +21,12 @@ def tile_bipartitegraph_kernel(tc, table, w1, vproj, b1, w2, b2, offs, out):
         tc.tile_pool(name="work", bufs=NV) as work,
         tc.psum_pool(name="psum", bufs=1) as psum,
     ):
+        table_sb = held.tile([K, S], BF16, name="table_sb")
+        nc.sync.dma_start(table_sb[:], table)
+        w1_sb = held.tile([K, BLOCKS, P], BF16, name="w1_sb")
+        nc.scalar.dma_start(w1_sb[:], w1.rearrange("k (i p) -> k i p", i=BLOCKS))
         offsets = held.tile([P, N // 16], U16, name="offsets")
         nc.sync.dma_start(offsets[:], offs)
-        table_sb = held.tile([K, S], BF16, name="table_sb")
-        nc.scalar.dma_start(table_sb[:], table)
-        w1_sb = held.tile([K, BLOCKS, P], BF16, name="w1_sb")
-        nc.sync.dma_start(w1_sb[:], w1.rearrange("k (i p) -> k i p", i=BLOCKS))
         vproj_sb = held.tile([P, BLOCKS, NV], F32, name="vproj_sb")
         nc.scalar.dma_start(vproj_sb[:], vproj.rearrange("(i p) t -> p i t", i=BLOCKS))
         b1_sb = held.tile([P, BLOCKS, 1], F32, name="b1_sb")
@@ -52,16 +51,12 @@ def tile_bipartitegraph_kernel(tc, table, w1, vproj, b1, w2, b2, offs, out):
             nc.vector.tensor_scalar(h[1][t][:], acc_h[1][t][:], bias1[:, 1, t : t + 1], 0.0, ADD, MAX)
 
         for t in range(NV):
-            acc_o = [psum.tile([Q, HALF], F32, name=f"acc_o{t}{s}", tag=f"acc_h{s}{t}") for s in range(2)]
-            for s in range(2):
-                for i in range(BLOCKS):
-                    nc.tensor.matmul(
-                        acc_o[s][:], w2_sb[:, i, :], h[i][t][:, s * HALF : (s + 1) * HALF],
-                        start=(i == 0), stop=(i == BLOCKS - 1),
-                    )
-            out_left = work.tile([Q, HALF], F32, name="out_left")
-            nc.scalar.activation(out_left[:], acc_o[0][:], RELU, bias=b2_sb[:, 0:1])
-            nc.scalar.dma_start(out[:, t * PIECE : t * PIECE + HALF], out_left[:])
-            out_right = work.tile([Q, HALF], F32, name="out_right")
-            nc.vector.tensor_scalar(out_right[:], acc_o[1][:], b2_sb[:, 0:1], 0.0, ADD, MAX)
-            nc.sync.dma_start(out[:, t * PIECE + HALF : (t + 1) * PIECE], out_right[:])
+            acc_o = psum.tile([Q, PIECE], F32, name=f"acc_o{t}", tag=f"acc_h0{t}")
+            for i in range(BLOCKS):
+                nc.tensor.matmul(acc_o[:], w2_sb[:, i, :], h[i][t][:], start=(i == 0), stop=(i == BLOCKS - 1))
+            out_sb = work.tile([Q, PIECE], F32, name="out_sb")
+            if t % 2 == 0:
+                nc.scalar.activation(out_sb[:], acc_o[:], RELU, bias=b2_sb[:, 0:1])
+            else:
+                nc.vector.tensor_scalar(out_sb[:], acc_o[:], b2_sb[:, 0:1], 0.0, ADD, MAX)
+            nc.sync.dma_start(out[:, t * PIECE : (t + 1) * PIECE], out_sb[:])

@@ -21,16 +21,16 @@ def tile_bipartitegraph_kernel(tc, table, w1, vproj, b1, w2, b2, offs, out):
         tc.tile_pool(name="work", bufs=NV) as work,
         tc.psum_pool(name="psum", bufs=1) as psum,
     ):
+        b1_sb = held.tile([P, BLOCKS, 1], F32, name="b1_sb")
+        nc.sync.dma_start(b1_sb[:], b1.rearrange("(i p) o -> p i o", i=BLOCKS))
+        vproj_sb = held.tile([P, BLOCKS, NV], F32, name="vproj_sb")
+        nc.scalar.dma_start(vproj_sb[:], vproj.rearrange("(i p) t -> p i t", i=BLOCKS))
         table_sb = held.tile([K, S], BF16, name="table_sb")
         nc.sync.dma_start(table_sb[:], table)
         w1_sb = held.tile([K, BLOCKS, P], BF16, name="w1_sb")
         nc.scalar.dma_start(w1_sb[:], w1.rearrange("k (i p) -> k i p", i=BLOCKS))
         offsets = held.tile([P, N // 16], U16, name="offsets")
         nc.sync.dma_start(offsets[:], offs)
-        vproj_sb = held.tile([P, BLOCKS, NV], F32, name="vproj_sb")
-        nc.scalar.dma_start(vproj_sb[:], vproj.rearrange("(i p) t -> p i t", i=BLOCKS))
-        b1_sb = held.tile([P, BLOCKS, 1], F32, name="b1_sb")
-        nc.sync.dma_start(b1_sb[:], b1.rearrange("(i p) o -> p i o", i=BLOCKS))
         w2_sb = held.tile([P, BLOCKS, Q], BF16, name="w2_sb")
         nc.scalar.dma_start(w2_sb[:], w2.rearrange("(i p) q -> p i q", i=BLOCKS))
         b2_sb = held.tile([Q, 1], F32, name="b2_sb")

@@ -11,6 +11,7 @@ N, NV = 1024, 4
 BLOCKS = R // P
 PIECE = N // NV
 COLS = PIECE // 16
+ROW32 = 8
 FLOPS = 2 * K * R * N + 2 * R * Q * N
 
 
@@ -21,10 +22,10 @@ def tile_bipartitegraph_kernel(tc, table, w1, vproj, b1, w2, b2, offs, out):
         tc.tile_pool(name="work", bufs=NV) as work,
         tc.psum_pool(name="psum", bufs=1) as psum,
     ):
-        b1_sb = held.tile([P, BLOCKS, 1], F32, name="b1_sb")
-        nc.sync.dma_start(b1_sb[:], b1.rearrange("(i p) o -> p i o", i=BLOCKS))
-        vproj_sb = held.tile([P, BLOCKS, NV], F32, name="vproj_sb")
-        nc.scalar.dma_start(vproj_sb[:], vproj.rearrange("(i p) t -> p i t", i=BLOCKS))
+        b1_sb = held.tile([P, BLOCKS, ROW32], F32, name="b1_sb")
+        nc.sync.dma_start(b1_sb[:, :, 0:1], b1.rearrange("(i p) o -> p i o", i=BLOCKS))
+        vproj_sb = held.tile([P, BLOCKS, ROW32], F32, name="vproj_sb")
+        nc.scalar.dma_start(vproj_sb[:, :, 0:NV], vproj.rearrange("(i p) t -> p i t", i=BLOCKS))
         table_sb = held.tile([K, S], BF16, name="table_sb")
         nc.sync.dma_start(table_sb[:], table)
         w1_sb = held.tile([K, BLOCKS, P], BF16, name="w1_sb")
@@ -37,7 +38,7 @@ def tile_bipartitegraph_kernel(tc, table, w1, vproj, b1, w2, b2, offs, out):
         nc.sync.dma_start(b2_sb[:], b2)
 
         bias1 = held.tile([P, BLOCKS, NV], F32, name="bias1")
-        nc.vector.tensor_tensor(bias1[:], vproj_sb[:], b1_sb[:].to_broadcast([P, BLOCKS, NV]), ADD)
+        nc.vector.tensor_tensor(bias1[:], vproj_sb[:, :, 0:NV], b1_sb[:, :, 0:1].to_broadcast([P, BLOCKS, NV]), ADD)
 
         acc_h = [[psum.tile([P, PIECE], F32, name=f"acc_h{i}{t}") for t in range(NV)] for i in range(BLOCKS)]
         for t in range(NV):

@@ -37,6 +37,11 @@ def tile_bipartitegraph_kernel(tc, table, w1, vproj, b1, w2, b2, offs, out):
         b2_sb = held.tile([Q, 1], F32, name="b2_sb")
         nc.sync.dma_start(b2_sb[:], b2)
 
+        zeros = held.tile([P, 1], F32, name="zeros")
+        nc.vector.memset(zeros[:], 0.0)
+        early = held.tile([P, 1], F32, name="early")
+        nc.scalar.activation(early[:], zeros[:], RELU)
+
         bias1 = held.tile([P, BLOCKS, NV], F32, name="bias1")
         nc.vector.tensor_tensor(bias1[:], vproj_sb[:, :, 0:NV], b1_sb[:, :, 0:1].to_broadcast([P, BLOCKS, NV]), ADD)
 

@@ -22,16 +22,16 @@ def tile_bipartitegraph_kernel(tc, table, w1, vproj, b1, w2, b2, offs, out):
         tc.tile_pool(name="work", bufs=NV) as work,
         tc.psum_pool(name="psum", bufs=1) as psum,
     ):
-        b1_sb = held.tile([P, BLOCKS, ROW32], F32, name="b1_sb")
-        nc.sync.dma_start(b1_sb[:, :, 0:1], b1.rearrange("(i p) o -> p i o", i=BLOCKS))
-        vproj_sb = held.tile([P, BLOCKS, ROW32], F32, name="vproj_sb")
-        nc.scalar.dma_start(vproj_sb[:, :, 0:NV], vproj.rearrange("(i p) t -> p i t", i=BLOCKS))
         table_sb = held.tile([K, S], BF16, name="table_sb")
         nc.sync.dma_start(table_sb[:], table)
         w1_sb = held.tile([K, BLOCKS, P], BF16, name="w1_sb")
         nc.scalar.dma_start(w1_sb[:], w1.rearrange("k (i p) -> k i p", i=BLOCKS))
         offsets = held.tile([P, N // 16], U16, name="offsets")
         nc.sync.dma_start(offsets[:], offs)
+        vproj_sb = held.tile([P, BLOCKS, ROW32], F32, name="vproj_sb")
+        nc.scalar.dma_start(vproj_sb[:, :, 0:NV], vproj.rearrange("(i p) t -> p i t", i=BLOCKS))
+        b1_sb = held.tile([P, BLOCKS, ROW32], F32, name="b1_sb")
+        nc.sync.dma_start(b1_sb[:, :, 0:1], b1.rearrange("(i p) o -> p i o", i=BLOCKS))
         w2_sb = held.tile([P, BLOCKS, Q], BF16, name="w2_sb")
         nc.scalar.dma_start(w2_sb[:], w2.rearrange("(i p) q -> p i q", i=BLOCKS))
         b2_sb = held.tile([Q, 1], F32, name="b2_sb")

@@ -11,6 +11,7 @@ N, NV = 1024, 4
 BLOCKS = R // P
 PIECE = N // NV
 COLS = PIECE // 16
+HALF = PIECE // 2
 ROW32 = 8
 FLOPS = 2 * K * R * N + 2 * R * Q * N
 
@@ -57,12 +58,19 @@ def tile_bipartitegraph_kernel(tc, table, w1, vproj, b1, w2, b2, offs, out):
             nc.vector.tensor_scalar(h[1][t][:], acc_h[1][t][:], bias1[:, 1, t : t + 1], 0.0, ADD, MAX)
 
         for t in range(NV):
-            acc_o = psum.tile([Q, PIECE], F32, name=f"acc_o{t}", tag=f"acc_h0{t}")
-            for i in range(BLOCKS):
-                nc.tensor.matmul(acc_o[:], w2_sb[:, i, :], h[i][t][:], start=(i == 0), stop=(i == BLOCKS - 1))
             out_sb = work.tile([Q, PIECE], F32, name="out_sb")
-            if t % 2 == 0:
-                nc.scalar.activation(out_sb[:], acc_o[:], RELU, bias=b2_sb[:, 0:1])
-            else:
-                nc.vector.tensor_scalar(out_sb[:], acc_o[:], b2_sb[:, 0:1], 0.0, ADD, MAX)
-            nc.sync.dma_start(out[:, t * PIECE : (t + 1) * PIECE], out_sb[:])
+            for s in range(2):
+                acc_o = psum.tile([Q, HALF], F32, name=f"acc_o{s}{t}", tag=f"acc_h{s}{t}")
+                for i in range(BLOCKS):
+                    nc.tensor.matmul(
+                        acc_o[:], w2_sb[:, i, :], h[i][t][:, s * HALF : (s + 1) * HALF], start=(i == 0), stop=(i == BLOCKS - 1)
+                    )
+                if s == 0:
+                    nc.scalar.activation(out_sb[:, 0:HALF], acc_o[:], RELU, bias=b2_sb[:, 0:1])
+                else:
+                    nc.vector.tensor_scalar(out_sb[:, HALF:PIECE], acc_o[:], b2_sb[:, 0:1], 0.0, ADD, MAX)
+                if t == NV - 1:
+                    first = t * PIECE + s * HALF
+                    nc.sync.dma_start(out[:, first : first + HALF], out_sb[:, s * HALF : (s + 1) * HALF])
+            if t < NV - 1:
+                nc.sync.dma_start(out[:, t * PIECE : (t + 1) * PIECE], out_sb[:])

@@ -69,8 +69,4 @@ def tile_bipartitegraph_kernel(tc, table, w1, vproj, b1, w2, b2, offs, out):
                     nc.scalar.activation(out_sb[:, 0:HALF], acc_o[:], RELU, bias=b2_sb[:, 0:1])
                 else:
                     nc.vector.tensor_scalar(out_sb[:, HALF:PIECE], acc_o[:], b2_sb[:, 0:1], 0.0, ADD, MAX)
-                if t == NV - 1:
-                    first = t * PIECE + s * HALF
-                    nc.sync.dma_start(out[:, first : first + HALF], out_sb[:, s * HALF : (s + 1) * HALF])
-            if t < NV - 1:
-                nc.sync.dma_start(out[:, t * PIECE : (t + 1) * PIECE], out_sb[:])
+            nc.sync.dma_start(out[:, t * PIECE : (t + 1) * PIECE], out_sb[:])

@@ -65,8 +65,9 @@ def tile_bipartitegraph_kernel(tc, table, w1, vproj, b1, w2, b2, offs, out):
                     nc.tensor.matmul(
                         acc_o[:], w2_sb[:, i, :], h[i][t][:, s * HALF : (s + 1) * HALF], start=(i == 0), stop=(i == BLOCKS - 1)
                     )
-                if s == 0:
-                    nc.scalar.activation(out_sb[:, 0:HALF], acc_o[:], RELU, bias=b2_sb[:, 0:1])
+                half = out_sb[:, s * HALF : (s + 1) * HALF]
+                if t % 2 == 0:
+                    nc.scalar.activation(half, acc_o[:], RELU, bias=b2_sb[:, 0:1])
                 else:
-                    nc.vector.tensor_scalar(out_sb[:, HALF:PIECE], acc_o[:], b2_sb[:, 0:1], 0.0, ADD, MAX)
+                    nc.vector.tensor_scalar(half, acc_o[:], b2_sb[:, 0:1], 0.0, ADD, MAX)
             nc.sync.dma_start(out[:, t * PIECE : (t + 1) * PIECE], out_sb[:])

@@ -54,8 +54,8 @@ def tile_bipartitegraph_kernel(tc, table, w1, vproj, b1, w2, b2, offs, out):
 
         h = [[work.tile([P, PIECE], BF16, name=f"h{i}") for t in range(NV)] for i in range(BLOCKS)]
         for t in range(NV):
-            nc.scalar.activation(h[0][t][:], acc_h[0][t][:], RELU, bias=bias1[:, 0, t : t + 1])
-            nc.vector.tensor_scalar(h[1][t][:], acc_h[1][t][:], bias1[:, 1, t : t + 1], 0.0, ADD, MAX)
+            nc.vector.tensor_scalar(h[0][t][:], acc_h[0][t][:], bias1[:, 0, t : t + 1], 0.0, ADD, MAX)
+            nc.scalar.activation(h[1][t][:], acc_h[1][t][:], RELU, bias=bias1[:, 1, t : t + 1])
 
         for t in range(NV):
             out_sb = work.tile([Q, PIECE], F32, name="out_sb")
@@ -66,8 +66,8 @@ def tile_bipartitegraph_kernel(tc, table, w1, vproj, b1, w2, b2, offs, out):
                         acc_o[:], w2_sb[:, i, :], h[i][t][:, s * HALF : (s + 1) * HALF], start=(i == 0), stop=(i == BLOCKS - 1)
                     )
                 half = out_sb[:, s * HALF : (s + 1) * HALF]
-                if t % 2 == 0:
-                    nc.scalar.activation(half, acc_o[:], RELU, bias=b2_sb[:, 0:1])
-                else:
+                if t in (0, NV - 1):
                     nc.vector.tensor_scalar(half, acc_o[:], b2_sb[:, 0:1], 0.0, ADD, MAX)
+                else:
+                    nc.scalar.activation(half, acc_o[:], RELU, bias=b2_sb[:, 0:1])
             nc.sync.dma_start(out[:, t * PIECE : (t + 1) * PIECE], out_sb[:])

@@ -34,7 +34,7 @@ def tile_bipartitegraph_kernel(tc, table, w1, vproj, b1, w2, b2, offs, out):
         b1_sb = held.tile([P, BLOCKS, ROW32], F32, name="b1_sb")
         nc.sync.dma_start(b1_sb[:, :, 0:1], b1.rearrange("(i p) o -> p i o", i=BLOCKS))
         w2_sb = held.tile([P, BLOCKS, Q], BF16, name="w2_sb")
-        nc.scalar.dma_start(w2_sb[:], w2.rearrange("(i p) q -> p i q", i=BLOCKS))
+        nc.sync.dma_start(w2_sb[:], w2.rearrange("(i p) q -> p i q", i=BLOCKS))
         b2_sb = held.tile([Q, 1], F32, name="b2_sb")
         nc.sync.dma_start(b2_sb[:], b2)
 

@@ -47,23 +47,26 @@ def tile_bipartitegraph_kernel(tc, table, w1, vproj, b1, w2, b2, offs, out):
         nc.vector.tensor_tensor(bias1[:], vproj_sb[:, :, 0:NV], b1_sb[:, :, 0:1].to_broadcast([P, BLOCKS, NV]), ADD)
 
         acc_h = [[psum.tile([P, PIECE], F32, name=f"acc_h{i}{t}") for t in range(NV)] for i in range(BLOCKS)]
-        for t in range(NV):
-            looked_up = table_sb[:].indirect(offsets[:, t * COLS : (t + 1) * COLS])
-            for i in range(BLOCKS):
+        for i in range(BLOCKS):
+            for t in range(NV):
+                looked_up = table_sb[:].indirect(offsets[:, t * COLS : (t + 1) * COLS])
                 nc.tensor.matmul(acc_h[i][t][:], w1_sb[:, i, :], looked_up, start=True, stop=True)
 
         h = [[work.tile([P, PIECE], BF16, name=f"h{i}") for t in range(NV)] for i in range(BLOCKS)]
-        for t in range(NV):
-            nc.vector.tensor_scalar(h[0][t][:], acc_h[0][t][:], bias1[:, 0, t : t + 1], 0.0, ADD, MAX)
-            nc.scalar.activation(h[1][t][:], acc_h[1][t][:], RELU, bias=bias1[:, 1, t : t + 1])
+        for i in range(BLOCKS):
+            for t in range(NV):
+                if t % 2 == 0:
+                    nc.vector.tensor_scalar(h[i][t][:], acc_h[i][t][:], bias1[:, i, t : t + 1], 0.0, ADD, MAX)
+                else:
+                    nc.scalar.activation(h[i][t][:], acc_h[i][t][:], RELU, bias=bias1[:, i, t : t + 1])
 
         for t in range(NV):
             out_sb = work.tile([Q, PIECE], F32, name="out_sb")
             for s in range(2):
                 acc_o = psum.tile([Q, HALF], F32, name=f"acc_o{s}{t}", tag=f"acc_h{s}{t}")
-                for i in range(BLOCKS):
+                for i in reversed(range(BLOCKS)):
                     nc.tensor.matmul(
-                        acc_o[:], w2_sb[:, i, :], h[i][t][:, s * HALF : (s + 1) * HALF], start=(i == 0), stop=(i == BLOCKS - 1)
+                        acc_o[:], w2_sb[:, i, :], h[i][t][:, s * HALF : (s + 1) * HALF], start=(i == BLOCKS - 1), stop=(i == 0)
                     )
                 half = out_sb[:, s * HALF : (s + 1) * HALF]
                 if t in (0, NV - 1):

@@ -26,11 +26,12 @@ def tile_bipartitegraph_kernel(tc, table, w1, vproj, b1, w2, b2, offs, out):
         table_sb = held.tile([K, S], BF16, name="table_sb")
         nc.sync.dma_start(table_sb[:], table)
         w1_sb = held.tile([K, BLOCKS, P], BF16, name="w1_sb")
-        nc.scalar.dma_start(w1_sb[:], w1.rearrange("k (i p) -> k i p", i=BLOCKS))
+        nc.scalar.dma_start(w1_sb[:, 0, :], w1[:, 0:P])
         offsets = held.tile([P, N // 16], U16, name="offsets")
         nc.sync.dma_start(offsets[:], offs)
         vproj_sb = held.tile([P, BLOCKS, ROW32], F32, name="vproj_sb")
         nc.scalar.dma_start(vproj_sb[:, :, 0:NV], vproj.rearrange("(i p) t -> p i t", i=BLOCKS))
+        nc.scalar.dma_start(w1_sb[:, 1, :], w1[:, P:R])
         b1_sb = held.tile([P, BLOCKS, ROW32], F32, name="b1_sb")
         nc.sync.dma_start(b1_sb[:, :, 0:1], b1.rearrange("(i p) o -> p i o", i=BLOCKS))
         w2_sb = held.tile([P, BLOCKS, Q], BF16, name="w2_sb")

import concourse.mybir as mybir

BF16, F32, U16 = mybir.dt.bfloat16, mybir.dt.float32, mybir.dt.uint16
ADD, MAX = mybir.AluOpType.add, mybir.AluOpType.max
RELU = mybir.ActivationFunctionType.Relu

P = 128
K, S = 128, 256
R, Q = 256, 128
N, NV = 1024, 4
BLOCKS = R // P
PIECE = N // NV
COLS = PIECE // 16
HALF = PIECE // 2
ROW32 = 8
FLOPS = 2 * K * R * N + 2 * R * Q * N


def tile_bipartitegraph_kernel(tc, table, w1, vproj, b1, w2, b2, offs, out):
    nc = tc.nc
    with (
        tc.tile_pool(name="held", bufs=1) as held,
        tc.tile_pool(name="work", bufs=NV) as work,
        tc.psum_pool(name="psum", bufs=1) as psum,
    ):
        table_sb = held.tile([K, S], BF16, name="table_sb")
        nc.sync.dma_start(table_sb[:], table)
        w1_sb = held.tile([K, BLOCKS, P], BF16, name="w1_sb")
        nc.scalar.dma_start(w1_sb[:, 0, :], w1[:, 0:P])
        offsets = held.tile([P, N // 16], U16, name="offsets")
        nc.sync.dma_start(offsets[:], offs)
        vproj_sb = held.tile([P, BLOCKS, ROW32], F32, name="vproj_sb")
        nc.scalar.dma_start(vproj_sb[:, :, 0:NV], vproj.rearrange("(i p) t -> p i t", i=BLOCKS))
        nc.scalar.dma_start(w1_sb[:, 1, :], w1[:, P:R])
        b1_sb = held.tile([P, BLOCKS, ROW32], F32, name="b1_sb")
        nc.sync.dma_start(b1_sb[:, :, 0:1], b1.rearrange("(i p) o -> p i o", i=BLOCKS))
        w2_sb = held.tile([P, BLOCKS, Q], BF16, name="w2_sb")
        nc.sync.dma_start(w2_sb[:], w2.rearrange("(i p) q -> p i q", i=BLOCKS))
        b2_sb = held.tile([Q, 1], F32, name="b2_sb")
        nc.sync.dma_start(b2_sb[:], b2)

        zeros = held.tile([P, 1], F32, name="zeros")
        nc.vector.memset(zeros[:], 0.0)
        early = held.tile([P, 1], F32, name="early")
        nc.scalar.activation(early[:], zeros[:], RELU)

        bias1 = held.tile([P, BLOCKS, NV], F32, name="bias1")
        nc.vector.tensor_tensor(bias1[:], vproj_sb[:, :, 0:NV], b1_sb[:, :, 0:1].to_broadcast([P, BLOCKS, NV]), ADD)

        acc_h = [[psum.tile([P, PIECE], F32, name=f"acc_h{i}{t}") for t in range(NV)] for i in range(BLOCKS)]
        for i in range(BLOCKS):
            for t in range(NV):
                looked_up = table_sb[:].indirect(offsets[:, t * COLS : (t + 1) * COLS])
                nc.tensor.matmul(acc_h[i][t][:], w1_sb[:, i, :], looked_up, start=True, stop=True)

        h = [[work.tile([P, PIECE], BF16, name=f"h{i}") for t in range(NV)] for i in range(BLOCKS)]
        for i in range(BLOCKS):
            for t in range(NV):
                if t % 2 == 0:
                    nc.vector.tensor_scalar(h[i][t][:], acc_h[i][t][:], bias1[:, i, t : t + 1], 0.0, ADD, MAX)
                else:
                    nc.scalar.activation(h[i][t][:], acc_h[i][t][:], RELU, bias=bias1[:, i, t : t + 1])

        for t in range(NV):
            out_sb = work.tile([Q, PIECE], F32, name="out_sb")
            for s in range(2):
                acc_o = psum.tile([Q, HALF], F32, name=f"acc_o{s}{t}", tag=f"acc_h{s}{t}")
                for i in reversed(range(BLOCKS)):
                    nc.tensor.matmul(
                        acc_o[:], w2_sb[:, i, :], h[i][t][:, s * HALF : (s + 1) * HALF], start=(i == BLOCKS - 1), stop=(i == 0)
                    )
                half = out_sb[:, s * HALF : (s + 1) * HALF]
                if t in (0, NV - 1):
                    nc.vector.tensor_scalar(half, acc_o[:], b2_sb[:, 0:1], 0.0, ADD, MAX)
                else:
                    nc.scalar.activation(half, acc_o[:], RELU, bias=b2_sb[:, 0:1])
            nc.sync.dma_start(out[:, t * PIECE : (t + 1) * PIECE], out_sb[:])
